import numpy as np
import ml_dtypes

BF16 = ml_dtypes.bfloat16


def bf(x):
    return np.asarray(x, np.float32).astype(BF16)


def f32(x):
    return np.asarray(x, np.float32)


def f64(x):
    return np.asarray(x).astype(np.float64)


def striped(idx):
    return np.tile(idx.reshape(-1, 16).T, (8, 1))


S, D, M, N = 4096, 128, 512, 1024


def setup_inputs():
    row_scale = 0.04 + 0.12 * np.random.random_sample((S, 1))
    return {"table": bf(row_scale * np.random.standard_normal((S, D))), "w": bf(np.random.standard_normal((D, M))), "b": f32(0.1 * np.random.standard_normal((M, 1))), "offs": striped(np.random.permutation(np.tile(np.arange(S), 2))[:N])}


def reference(table, w, b, offs):
    idx = offs[:16].T.reshape(-1)
    t = f64(table)
    nrm = np.sqrt(np.sum(t * t, axis=1, keepdims=True))
    ehat = t * np.minimum(1.0, 1.0 / nrm)
    return f64(w).T @ ehat[idx].T + f64(b)

@@ -1,0 +1,93 @@
+import concourse.masks as masks
+import concourse.mybir as mybir
+
+BF16, F32, U16 = mybir.dt.bfloat16, mybir.dt.float32, mybir.dt.uint16
+ACT = mybir.ActivationFunctionType
+
+P = 128
+S, D, M, N = 4096, 128, 512, 1024
+BLOCKS = S // P
+CHUNK = 4
+PIECE = 512
+LAYERS = M // P
+
+FLOPS = 2 * D * M * N
+
+
+def tile_gatv2model_kernel(tc, table, w, b, offs, out):
+    nc = tc.nc
+    table_blocks = table.rearrange("(c p) d -> p c d", p=P)
+    b_by_layer = b.rearrange("(l p) o -> l (p o)", p=P)
+
+    with (
+        tc.tile_pool(name="held", bufs=1) as held,
+        tc.tile_pool(name="loaded", bufs=BLOCKS // CHUNK) as loaded,
+        tc.tile_pool(name="work", bufs=3) as work,
+        tc.tile_pool(name="staged", bufs=4) as staged,
+        tc.psum_pool(name="flipped", bufs=3) as flipped,
+        tc.psum_pool(name="small", bufs=1) as small,
+        tc.psum_pool(name="products", bufs=4) as products,
+    ):
+        raw_chunks = []
+        for k in range(BLOCKS // CHUNK):
+            raw = loaded.tile([P, CHUNK, D], BF16, name="raw")
+            nc.sync.dma_start(raw[:], table_blocks[:, k * CHUNK : (k + 1) * CHUNK, :])
+            raw_chunks.append(raw)
+        offsets = held.tile([P, N // 16], U16, name="offsets")
+        nc.sync.dma_start(offsets[:], offs)
+        weights = held.tile([P, M], BF16, name="weights")
+        nc.gpsimd.dma_start(weights[:], w)
+        bias_rows = held.tile([LAYERS, P], F32, name="bias_rows")
+        nc.gpsimd.dma_start(bias_rows[:], b_by_layer)
+
+        identity = held.tile([P, P], BF16, name="identity")
+        masks.make_identity(nc, identity[:])
+        identity_f32 = held.tile([LAYERS, LAYERS], F32, name="identity_f32")
+        masks.make_identity(nc, identity_f32[:])
+
+        bias_turned = small.tile([P, LAYERS], F32, name="bias_turned")
+        nc.tensor.matmul(bias_turned[:], bias_rows[:], identity_f32[:], start=True, stop=True)
+        bias = held.tile([P, LAYERS], F32, name="bias")
+        nc.vector.tensor_copy(bias[:], bias_turned[:])
+
+        window = held.tile([P, S], BF16, name="window")
+        for k, raw in enumerate(raw_chunks):
+            sumsq = work.tile([P, CHUNK], F32, name="sumsq")
+            for c in range(CHUNK):
+                squares = work.tile([P, D], BF16, name="squares")
+                nc.scalar.activation(
+                    squares[:], raw[:, c, :], ACT.Square, accum_out=sumsq[:, c : c + 1]
+                )
+            inv_norm = work.tile([P, CHUNK], F32, name="inv_norm")
+            nc.scalar.activation(inv_norm[:], sumsq[:], ACT.Abs_reciprocal_sqrt)
+            scale = work.tile([P, CHUNK], F32, name="scale")
+            nc.vector.tensor_scalar_min(scale[:], inv_norm[:], 1.0)
+            clipped = work.tile([P, CHUNK, D], BF16, name="clipped")
+            for c in range(CHUNK):
+                nc.vector.tensor_scalar_mul(clipped[:, c, :], raw[:, c, :], scale[:, c : c + 1])
+            turned = flipped.tile([P, CHUNK * P], BF16, name="turned")
+            for c in range(CHUNK):
+                nc.tensor.transpose(turned[:, c * P : (c + 1) * P], clipped[:, c, :], identity[:])
+            nc.vector.tensor_copy(window[:, k * CHUNK * P : (k + 1) * CHUNK * P], turned[:])
+
+        for layer in range(LAYERS):
+            for piece in range(N // PIECE):
+                picked = window[:].indirect(
+                    offsets[:, piece * (PIECE // 16) : (piece + 1) * (PIECE // 16)]
+                )
+                product = products.tile([P, PIECE], F32, name="product")
+                nc.tensor.matmul(
+                    product[:], weights[:, layer * P : (layer + 1) * P], picked,
+                    start=True, stop=True,
+                )
+                result = staged.tile([P, PIECE], F32, name="result")
+                if piece % 2 == 0:
+                    nc.vector.tensor_scalar_add(result[:], product[:], bias[:, layer : layer + 1])
+                else:
+                    nc.scalar.activation(
+                        result[:], product[:], ACT.Identity, bias=bias[:, layer : layer + 1]
+                    )
+                nc.sync.dma_start(
+                    out[layer * P : (layer + 1) * P, piece * PIECE : (piece + 1) * PIECE],
+                    result[:],
+                )

@@ -67,7 +67,10 @@ def tile_gatv2model_kernel(tc, table, w, b, offs, out):
                 nc.vector.tensor_scalar_mul(clipped[:, c, :], raw[:, c, :], scale[:, c : c + 1])
             turned = flipped.tile([P, CHUNK * P], BF16, name="turned")
             for c in range(CHUNK):
-                nc.tensor.transpose(turned[:, c * P : (c + 1) * P], clipped[:, c, :], identity[:])
+                nc.tensor.matmul(
+                    turned[:, c * P : (c + 1) * P], clipped[:, c, :], identity[:],
+                    start=True, stop=True,
+                )
             nc.vector.tensor_copy(window[:, k * CHUNK * P : (k + 1) * CHUNK * P], turned[:])
 
         for layer in range(LAYERS):

@@ -3,6 +3,7 @@ import concourse.mybir as mybir
 
 BF16, F32, U16 = mybir.dt.bfloat16, mybir.dt.float32, mybir.dt.uint16
 ACT = mybir.ActivationFunctionType
+ALU = mybir.AluOpType
 
 P = 128
 S, D, M, N = 4096, 128, 512, 1024
@@ -36,14 +37,18 @@ def tile_gatv2model_kernel(tc, table, w, b, offs, out):
         offsets = held.tile([P, N // 16], U16, name="offsets")
         nc.sync.dma_start(offsets[:], offs)
         weights = held.tile([P, M], BF16, name="weights")
-        nc.gpsimd.dma_start(weights[:], w)
+        nc.sync.dma_start(weights[:], w)
         bias_rows = held.tile([LAYERS, P], F32, name="bias_rows")
-        nc.gpsimd.dma_start(bias_rows[:], b_by_layer)
+        nc.sync.dma_start(bias_rows[:], b_by_layer)
 
         identity = held.tile([P, P], BF16, name="identity")
         masks.make_identity(nc, identity[:])
         identity_f32 = held.tile([LAYERS, LAYERS], F32, name="identity_f32")
         masks.make_identity(nc, identity_f32[:])
+
+        scratch = held.tile([P, 1], F32, name="scratch")
+        nc.vector.memset(scratch[:], 1.0)
+        nc.scalar.activation(scratch[:], scratch[:], ACT.Abs_reciprocal_sqrt)
 
         bias_turned = small.tile([P, LAYERS], F32, name="bias_turned")
         nc.tensor.matmul(bias_turned[:], bias_rows[:], identity_f32[:], start=True, stop=True)
@@ -54,10 +59,17 @@ def tile_gatv2model_kernel(tc, table, w, b, offs, out):
         for k, raw in enumerate(raw_chunks):
             sumsq = work.tile([P, CHUNK], F32, name="sumsq")
             for c in range(CHUNK):
-                squares = work.tile([P, D], BF16, name="squares")
-                nc.scalar.activation(
-                    squares[:], raw[:, c, :], ACT.Square, accum_out=sumsq[:, c : c + 1]
-                )
+                if k % 4 == 1:
+                    squares_v = work.tile([P, D], F32, name="squares_v")
+                    nc.vector.scalar_tensor_tensor(
+                        squares_v[:], raw[:, c, :], 1.0, raw[:, c, :], ALU.mult, ALU.mult,
+                        accum_out=sumsq[:, c : c + 1],
+                    )
+                else:
+                    squares_s = work.tile([P, D], BF16, name="squares_s")
+                    nc.scalar.activation(
+                        squares_s[:], raw[:, c, :], ACT.Square, accum_out=sumsq[:, c : c + 1]
+                    )
             inv_norm = work.tile([P, CHUNK], F32, name="inv_norm")
             nc.scalar.activation(inv_norm[:], sumsq[:], ACT.Abs_reciprocal_sqrt)
             scale = work.tile([P, CHUNK], F32, name="scale")

@@ -7,8 +7,8 @@ ALU = mybir.AluOpType
 
 P = 128
 S, D, M, N = 4096, 128, 512, 1024
-BLOCKS = S // P
 CHUNK = 4
+CHUNKS = S // (CHUNK * P)
 PIECE = 512
 LAYERS = M // P
 
@@ -17,23 +17,19 @@ FLOPS = 2 * D * M * N
 
 def tile_gatv2model_kernel(tc, table, w, b, offs, out):
     nc = tc.nc
-    table_blocks = table.rearrange("(c p) d -> p c d", p=P)
+    table_chunks = table.rearrange("(k c p) d -> k p c d", c=CHUNK, p=P)
     b_by_layer = b.rearrange("(l p) o -> l (p o)", p=P)
 
     with (
         tc.tile_pool(name="held", bufs=1) as held,
-        tc.tile_pool(name="loaded", bufs=BLOCKS // CHUNK) as loaded,
-        tc.tile_pool(name="work", bufs=3) as work,
-        tc.tile_pool(name="staged", bufs=4) as staged,
-        tc.psum_pool(name="flipped", bufs=3) as flipped,
-        tc.psum_pool(name="small", bufs=1) as small,
+        tc.tile_pool(name="work", bufs=CHUNKS) as work,
+        tc.tile_pool(name="staged", bufs=LAYERS * N // PIECE) as staged,
+        tc.psum_pool(name="flipped", bufs=4) as flipped,
         tc.psum_pool(name="products", bufs=4) as products,
     ):
-        raw_chunks = []
-        for k in range(BLOCKS // CHUNK):
-            raw = loaded.tile([P, CHUNK, D], BF16, name="raw")
-            nc.sync.dma_start(raw[:], table_blocks[:, k * CHUNK : (k + 1) * CHUNK, :])
-            raw_chunks.append(raw)
+        raw = [held.tile([P, CHUNK, D], BF16, name=f"raw{k}") for k in range(CHUNKS)]
+        for k in range(CHUNKS):
+            nc.sync.dma_start(raw[k][:], table_chunks[k])
         offsets = held.tile([P, N // 16], U16, name="offsets")
         nc.sync.dma_start(offsets[:], offs)
         weights = held.tile([P, M], BF16, name="weights")
@@ -50,40 +46,56 @@ def tile_gatv2model_kernel(tc, table, w, b, offs, out):
         nc.vector.memset(scratch[:], 1.0)
         nc.scalar.activation(scratch[:], scratch[:], ACT.Abs_reciprocal_sqrt)
 
-        bias_turned = small.tile([P, LAYERS], F32, name="bias_turned")
-        nc.tensor.matmul(bias_turned[:], bias_rows[:], identity_f32[:], start=True, stop=True)
-        bias = held.tile([P, LAYERS], F32, name="bias")
-        nc.vector.tensor_copy(bias[:], bias_turned[:])
-
         window = held.tile([P, S], BF16, name="window")
-        for k, raw in enumerate(raw_chunks):
-            sumsq = work.tile([P, CHUNK], F32, name="sumsq")
+        sumsq = [None] * CHUNKS
+        turned = [None] * CHUNKS
+
+        def add_up_squares(k):
+            sumsq[k] = work.tile([P, CHUNK], F32, name="sumsq")
             for c in range(CHUNK):
                 if k % 4 == 1:
                     squares_v = work.tile([P, D], F32, name="squares_v")
                     nc.vector.scalar_tensor_tensor(
-                        squares_v[:], raw[:, c, :], 1.0, raw[:, c, :], ALU.mult, ALU.mult,
-                        accum_out=sumsq[:, c : c + 1],
+                        squares_v[:], raw[k][:, c, :], 1.0, raw[k][:, c, :], ALU.mult, ALU.mult,
+                        accum_out=sumsq[k][:, c : c + 1],
                     )
                 else:
                     squares_s = work.tile([P, D], BF16, name="squares_s")
                     nc.scalar.activation(
-                        squares_s[:], raw[:, c, :], ACT.Square, accum_out=sumsq[:, c : c + 1]
+                        squares_s[:], raw[k][:, c, :], ACT.Square,
+                        accum_out=sumsq[k][:, c : c + 1],
                     )
+
+        def clip_and_turn(k):
             inv_norm = work.tile([P, CHUNK], F32, name="inv_norm")
-            nc.scalar.activation(inv_norm[:], sumsq[:], ACT.Abs_reciprocal_sqrt)
+            nc.scalar.activation(inv_norm[:], sumsq[k][:], ACT.Abs_reciprocal_sqrt)
             scale = work.tile([P, CHUNK], F32, name="scale")
             nc.vector.tensor_scalar_min(scale[:], inv_norm[:], 1.0)
             clipped = work.tile([P, CHUNK, D], BF16, name="clipped")
             for c in range(CHUNK):
-                nc.vector.tensor_scalar_mul(clipped[:, c, :], raw[:, c, :], scale[:, c : c + 1])
-            turned = flipped.tile([P, CHUNK * P], BF16, name="turned")
+                nc.vector.tensor_scalar_mul(clipped[:, c, :], raw[k][:, c, :], scale[:, c : c + 1])
+            turned[k] = flipped.tile([P, CHUNK * P], BF16, name="turned")
             for c in range(CHUNK):
                 nc.tensor.matmul(
-                    turned[:, c * P : (c + 1) * P], clipped[:, c, :], identity[:],
+                    turned[k][:, c * P : (c + 1) * P], clipped[:, c, :], identity[:],
                     start=True, stop=True,
                 )
-            nc.vector.tensor_copy(window[:, k * CHUNK * P : (k + 1) * CHUNK * P], turned[:])
+
+        def fill_window(k):
+            nc.vector.tensor_copy(window[:, k * CHUNK * P : (k + 1) * CHUNK * P], turned[k][:])
+
+        for i in range(CHUNKS + 2):
+            if i < CHUNKS:
+                add_up_squares(i)
+            if 1 <= i <= CHUNKS:
+                clip_and_turn(i - 1)
+            if i >= 2:
+                fill_window(i - 2)
+
+        bias_turned = flipped.tile([P, LAYERS], F32, name="bias_turned", tag="turned")
+        nc.tensor.matmul(bias_turned[:], bias_rows[:], identity_f32[:], start=True, stop=True)
+        bias = held.tile([P, LAYERS], F32, name="bias")
+        nc.vector.tensor_copy(bias[:], bias_turned[:])
 
         for layer in range(LAYERS):
             for piece in range(N // PIECE):

@@ -24,7 +24,8 @@ def tile_gatv2model_kernel(tc, table, w, b, offs, out):
         tc.tile_pool(name="held", bufs=1) as held,
         tc.tile_pool(name="work", bufs=CHUNKS) as work,
         tc.tile_pool(name="staged", bufs=LAYERS * N // PIECE) as staged,
-        tc.psum_pool(name="flipped", bufs=4) as flipped,
+        tc.psum_pool(name="flipped", bufs=3) as flipped,
+        tc.psum_pool(name="unread", bufs=1) as unread,
         tc.psum_pool(name="products", bufs=4) as products,
     ):
         raw = [held.tile([P, CHUNK, D], BF16, name=f"raw{k}") for k in range(CHUNKS)]
@@ -47,6 +48,7 @@ def tile_gatv2model_kernel(tc, table, w, b, offs, out):
         nc.scalar.activation(scratch[:], scratch[:], ACT.Abs_reciprocal_sqrt)
 
         window = held.tile([P, S], BF16, name="window")
+        thrown_away = unread.tile([P, CHUNK * D], F32, name="thrown_away")
         sumsq = [None] * CHUNKS
         turned = [None] * CHUNKS
 
@@ -80,6 +82,10 @@ def tile_gatv2model_kernel(tc, table, w, b, offs, out):
                     turned[k][:, c * P : (c + 1) * P], clipped[:, c, :], identity[:],
                     start=True, stop=True,
                 )
+            nc.tensor.matmul(
+                thrown_away[:], identity[:], raw[0][:].rearrange("p c d -> p (c d)"),
+                start=True, stop=True,
+            )
 
         def fill_window(k):
             nc.vector.tensor_copy(window[:, k * CHUNK * P : (k + 1) * CHUNK * P], turned[k][:])

@@ -24,8 +24,7 @@ def tile_gatv2model_kernel(tc, table, w, b, offs, out):
         tc.tile_pool(name="held", bufs=1) as held,
         tc.tile_pool(name="work", bufs=CHUNKS) as work,
         tc.tile_pool(name="staged", bufs=LAYERS * N // PIECE) as staged,
-        tc.psum_pool(name="flipped", bufs=3) as flipped,
-        tc.psum_pool(name="unread", bufs=1) as unread,
+        tc.psum_pool(name="flipped", bufs=4) as flipped,
         tc.psum_pool(name="products", bufs=4) as products,
     ):
         raw = [held.tile([P, CHUNK, D], BF16, name=f"raw{k}") for k in range(CHUNKS)]
@@ -48,14 +47,13 @@ def tile_gatv2model_kernel(tc, table, w, b, offs, out):
         nc.scalar.activation(scratch[:], scratch[:], ACT.Abs_reciprocal_sqrt)
 
         window = held.tile([P, S], BF16, name="window")
-        thrown_away = unread.tile([P, CHUNK * D], F32, name="thrown_away")
         sumsq = [None] * CHUNKS
         turned = [None] * CHUNKS
 
         def add_up_squares(k):
             sumsq[k] = work.tile([P, CHUNK], F32, name="sumsq")
             for c in range(CHUNK):
-                if k % 4 == 1:
+                if k % 3 == 1:
                     squares_v = work.tile([P, D], F32, name="squares_v")
                     nc.vector.scalar_tensor_tensor(
                         squares_v[:], raw[k][:, c, :], 1.0, raw[k][:, c, :], ALU.mult, ALU.mult,
@@ -82,10 +80,6 @@ def tile_gatv2model_kernel(tc, table, w, b, offs, out):
                     turned[k][:, c * P : (c + 1) * P], clipped[:, c, :], identity[:],
                     start=True, stop=True,
                 )
-            nc.tensor.matmul(
-                thrown_away[:], identity[:], raw[0][:].rearrange("p c d -> p (c d)"),
-                start=True, stop=True,
-            )
 
         def fill_window(k):
             nc.vector.tensor_copy(window[:, k * CHUNK * P : (k + 1) * CHUNK * P], turned[k][:])

@@ -23,7 +23,7 @@ def tile_gatv2model_kernel(tc, table, w, b, offs, out):
     with (
         tc.tile_pool(name="held", bufs=1) as held,
         tc.tile_pool(name="work", bufs=CHUNKS) as work,
-        tc.tile_pool(name="staged", bufs=LAYERS * N // PIECE) as staged,
+        tc.tile_pool(name="staged", bufs=LAYERS * N // PIECE + 2) as staged,
         tc.psum_pool(name="flipped", bufs=4) as flipped,
         tc.psum_pool(name="products", bufs=4) as products,
     ):
@@ -97,24 +97,25 @@ def tile_gatv2model_kernel(tc, table, w, b, offs, out):
         bias = held.tile([P, LAYERS], F32, name="bias")
         nc.vector.tensor_copy(bias[:], bias_turned[:])
 
+        pieces = []
         for layer in range(LAYERS):
-            for piece in range(N // PIECE):
-                picked = window[:].indirect(
-                    offsets[:, piece * (PIECE // 16) : (piece + 1) * (PIECE // 16)]
-                )
-                product = products.tile([P, PIECE], F32, name="product")
-                nc.tensor.matmul(
-                    product[:], weights[:, layer * P : (layer + 1) * P], picked,
-                    start=True, stop=True,
-                )
-                result = staged.tile([P, PIECE], F32, name="result")
-                if piece % 2 == 0:
-                    nc.vector.tensor_scalar_add(result[:], product[:], bias[:, layer : layer + 1])
+            for first in range(0, N, PIECE):
+                if (layer, first) in ((0, 0), (LAYERS - 1, N - PIECE)):
+                    pieces.append((layer, first, PIECE // 2))
+                    pieces.append((layer, first + PIECE // 2, PIECE // 2))
                 else:
-                    nc.scalar.activation(
-                        result[:], product[:], ACT.Identity, bias=bias[:, layer : layer + 1]
-                    )
-                nc.sync.dma_start(
-                    out[layer * P : (layer + 1) * P, piece * PIECE : (piece + 1) * PIECE],
-                    result[:],
+                    pieces.append((layer, first, PIECE))
+        for i, (layer, first, edges) in enumerate(pieces):
+            picked = window[:].indirect(offsets[:, first // 16 : (first + edges) // 16])
+            product = products.tile([P, edges], F32, name="product")
+            nc.tensor.matmul(
+                product[:], weights[:, layer * P : (layer + 1) * P], picked, start=True, stop=True
+            )
+            result = staged.tile([P, edges], F32, name="result")
+            if i % 2 == 0:
+                nc.vector.tensor_scalar_add(result[:], product[:], bias[:, layer : layer + 1])
+            else:
+                nc.scalar.activation(
+                    result[:], product[:], ACT.Identity, bias=bias[:, layer : layer + 1]
                 )
+            nc.sync.dma_start(out[layer * P : (layer + 1) * P, first : first + edges], result[:])

@@ -18,7 +18,7 @@ FLOPS = 2 * D * M * N
 def tile_gatv2model_kernel(tc, table, w, b, offs, out):
     nc = tc.nc
     table_chunks = table.rearrange("(k c p) d -> k p c d", c=CHUNK, p=P)
-    b_by_layer = b.rearrange("(l p) o -> l (p o)", p=P)
+    b_by_row = b.rearrange("(l p) o -> p (l o)", p=P)
 
     with (
         tc.tile_pool(name="held", bufs=1) as held,
@@ -34,13 +34,11 @@ def tile_gatv2model_kernel(tc, table, w, b, offs, out):
         nc.sync.dma_start(offsets[:], offs)
         weights = held.tile([P, M], BF16, name="weights")
         nc.sync.dma_start(weights[:], w)
-        bias_rows = held.tile([LAYERS, P], F32, name="bias_rows")
-        nc.sync.dma_start(bias_rows[:], b_by_layer)
+        bias = held.tile([P, LAYERS], F32, name="bias")
+        nc.sync.dma_start(bias[:], b_by_row)
 
         identity = held.tile([P, P], BF16, name="identity")
         masks.make_identity(nc, identity[:])
-        identity_f32 = held.tile([LAYERS, LAYERS], F32, name="identity_f32")
-        masks.make_identity(nc, identity_f32[:])
 
         scratch = held.tile([P, 1], F32, name="scratch")
         nc.vector.memset(scratch[:], 1.0)
@@ -91,11 +89,6 @@ def tile_gatv2model_kernel(tc, table, w, b, offs, out):
                 clip_and_turn(i - 1)
             if i >= 2:
                 fill_window(i - 2)
-
-        bias_turned = flipped.tile([P, LAYERS], F32, name="bias_turned", tag="turned")
-        nc.tensor.matmul(bias_turned[:], bias_rows[:], identity_f32[:], start=True, stop=True)
-        bias = held.tile([P, LAYERS], F32, name="bias")
-        nc.vector.tensor_copy(bias[:], bias_turned[:])
 
         pieces = []
         for layer in range(LAYERS):

@@ -28,7 +28,9 @@ def tile_gatv2model_kernel(tc, table, w, b, offs, out):
         tc.psum_pool(name="products", bufs=4) as products,
     ):
         raw = [held.tile([P, CHUNK, D], BF16, name=f"raw{k}") for k in range(CHUNKS)]
-        for k in range(CHUNKS):
+        for c in range(CHUNK):
+            nc.sync.dma_start(raw[0][:, c, :], table_chunks[0][:, c, :])
+        for k in range(1, CHUNKS):
             nc.sync.dma_start(raw[k][:], table_chunks[k])
         offsets = held.tile([P, N // 16], U16, name="offsets")
         nc.sync.dma_start(offsets[:], offs)
@@ -51,7 +53,7 @@ def tile_gatv2model_kernel(tc, table, w, b, offs, out):
         def add_up_squares(k):
             sumsq[k] = work.tile([P, CHUNK], F32, name="sumsq")
             for c in range(CHUNK):
-                if k % 3 == 1:
+                if (k % 3 == 1 and k < CHUNKS - 1) or (k == CHUNKS - 1 and c < CHUNK // 2):
                     squares_v = work.tile([P, D], F32, name="squares_v")
                     nc.vector.scalar_tensor_tensor(
                         squares_v[:], raw[k][:, c, :], 1.0, raw[k][:, c, :], ALU.mult, ALU.mult,
@@ -72,15 +74,23 @@ def tile_gatv2model_kernel(tc, table, w, b, offs, out):
             clipped = work.tile([P, CHUNK, D], BF16, name="clipped")
             for c in range(CHUNK):
                 nc.vector.tensor_scalar_mul(clipped[:, c, :], raw[k][:, c, :], scale[:, c : c + 1])
-            turned[k] = flipped.tile([P, CHUNK * P], BF16, name="turned")
-            for c in range(CHUNK):
-                nc.tensor.matmul(
-                    turned[k][:, c * P : (c + 1) * P], clipped[:, c, :], identity[:],
-                    start=True, stop=True,
-                )
+            tiles = 2 if k == CHUNKS - 1 else 1
+            blocks = CHUNK // tiles
+            turned[k] = []
+            for t in range(tiles):
+                turned_blocks = flipped.tile([P, blocks * P], BF16, name="turned_blocks", tag="turned")
+                for c in range(blocks):
+                    nc.tensor.matmul(
+                        turned_blocks[:, c * P : (c + 1) * P], clipped[:, t * blocks + c, :],
+                        identity[:], start=True, stop=True,
+                    )
+                turned[k].append(turned_blocks)
 
         def fill_window(k):
-            nc.vector.tensor_copy(window[:, k * CHUNK * P : (k + 1) * CHUNK * P], turned[k][:])
+            columns = CHUNK * P // len(turned[k])
+            for t, turned_blocks in enumerate(turned[k]):
+                first = k * CHUNK * P + t * columns
+                nc.vector.tensor_copy(window[:, first : first + columns], turned_blocks[:])
 
         for i in range(CHUNKS + 2):
             if i < CHUNKS:

@@ -53,7 +53,7 @@ def tile_gatv2model_kernel(tc, table, w, b, offs, out):
         def add_up_squares(k):
             sumsq[k] = work.tile([P, CHUNK], F32, name="sumsq")
             for c in range(CHUNK):
-                if (k % 3 == 1 and k < CHUNKS - 1) or (k == CHUNKS - 1 and c < CHUNK // 2):
+                if (c % 2 == 1) if k in (0, CHUNKS - 1) else (k % 3 == 1):
                     squares_v = work.tile([P, D], F32, name="squares_v")
                     nc.vector.scalar_tensor_tensor(
                         squares_v[:], raw[k][:, c, :], 1.0, raw[k][:, c, :], ALU.mult, ALU.mult,

@@ -42,9 +42,12 @@ def tile_gatv2model_kernel(tc, table, w, b, offs, out):
         identity = held.tile([P, P], BF16, name="identity")
         masks.make_identity(nc, identity[:])
 
+        one = held.tile([P, 1], F32, name="one")
+        nc.vector.memset(one[:], 1.0)
+        minus_one = held.tile([P, 1], F32, name="minus_one")
+        nc.vector.memset(minus_one[:], -1.0)
         scratch = held.tile([P, 1], F32, name="scratch")
-        nc.vector.memset(scratch[:], 1.0)
-        nc.scalar.activation(scratch[:], scratch[:], ACT.Abs_reciprocal_sqrt)
+        nc.scalar.activation(scratch[:], one[:], ACT.Abs_reciprocal_sqrt)
 
         window = held.tile([P, S], BF16, name="window")
         sumsq = [None] * CHUNKS
@@ -53,7 +56,7 @@ def tile_gatv2model_kernel(tc, table, w, b, offs, out):
         def add_up_squares(k):
             sumsq[k] = work.tile([P, CHUNK], F32, name="sumsq")
             for c in range(CHUNK):
-                if (c % 2 == 1) if k in (0, CHUNKS - 1) else (k % 3 == 1):
+                if (c % 2 == 1) if k in (0, CHUNKS - 1) else (c == CHUNK - 1):
                     squares_v = work.tile([P, D], F32, name="squares_v")
                     nc.vector.scalar_tensor_tensor(
                         squares_v[:], raw[k][:, c, :], 1.0, raw[k][:, c, :], ALU.mult, ALU.mult,
@@ -67,10 +70,10 @@ def tile_gatv2model_kernel(tc, table, w, b, offs, out):
                     )
 
         def clip_and_turn(k):
-            inv_norm = work.tile([P, CHUNK], F32, name="inv_norm")
-            nc.scalar.activation(inv_norm[:], sumsq[k][:], ACT.Abs_reciprocal_sqrt)
+            excess = work.tile([P, CHUNK], F32, name="excess")
+            nc.scalar.activation(excess[:], sumsq[k][:], ACT.Relu, bias=minus_one[:])
             scale = work.tile([P, CHUNK], F32, name="scale")
-            nc.vector.tensor_scalar_min(scale[:], inv_norm[:], 1.0)
+            nc.scalar.activation(scale[:], excess[:], ACT.Abs_reciprocal_sqrt, bias=one[:])
             clipped = work.tile([P, CHUNK, D], BF16, name="clipped")
             for c in range(CHUNK):
                 nc.vector.tensor_scalar_mul(clipped[:, c, :], raw[k][:, c, :], scale[:, c : c + 1])

@@ -9,7 +9,7 @@ P = 128
 S, D, M, N = 4096, 128, 512, 1024
 CHUNK = 4
 CHUNKS = S // (CHUNK * P)
-PIECE = 512
+PIECE = 256
 LAYERS = M // P
 
 FLOPS = 2 * D * M * N
@@ -23,9 +23,8 @@ def tile_gatv2model_kernel(tc, table, w, b, offs, out):
     with (
         tc.tile_pool(name="held", bufs=1) as held,
         tc.tile_pool(name="work", bufs=CHUNKS) as work,
-        tc.tile_pool(name="staged", bufs=LAYERS * N // PIECE + 2) as staged,
-        tc.psum_pool(name="flipped", bufs=4) as flipped,
-        tc.psum_pool(name="products", bufs=4) as products,
+        tc.tile_pool(name="staged", bufs=LAYERS * N // (2 * PIECE)) as staged,
+        tc.psum_pool(name="banks", bufs=8) as banks,
     ):
         raw = [held.tile([P, CHUNK, D], BF16, name=f"raw{k}") for k in range(CHUNKS)]
         for c in range(CHUNK):
@@ -81,7 +80,7 @@ def tile_gatv2model_kernel(tc, table, w, b, offs, out):
             blocks = CHUNK // tiles
             turned[k] = []
             for t in range(tiles):
-                turned_blocks = flipped.tile([P, blocks * P], BF16, name="turned_blocks", tag="turned")
+                turned_blocks = banks.tile([P, blocks * P], BF16, name="turned_blocks", tag="bank")
                 for c in range(blocks):
                     nc.tensor.matmul(
                         turned_blocks[:, c * P : (c + 1) * P], clipped[:, t * blocks + c, :],
@@ -103,25 +102,26 @@ def tile_gatv2model_kernel(tc, table, w, b, offs, out):
             if i >= 2:
                 fill_window(i - 2)
 
-        pieces = []
-        for layer in range(LAYERS):
-            for first in range(0, N, PIECE):
-                if (layer, first) in ((0, 0), (LAYERS - 1, N - PIECE)):
-                    pieces.append((layer, first, PIECE // 2))
-                    pieces.append((layer, first + PIECE // 2, PIECE // 2))
-                else:
-                    pieces.append((layer, first, PIECE))
-        for i, (layer, first, edges) in enumerate(pieces):
-            picked = window[:].indirect(offsets[:, first // 16 : (first + edges) // 16])
-            product = products.tile([P, edges], F32, name="product")
-            nc.tensor.matmul(
-                product[:], weights[:, layer * P : (layer + 1) * P], picked, start=True, stop=True
-            )
-            result = staged.tile([P, edges], F32, name="result")
-            if i % 2 == 0:
-                nc.vector.tensor_scalar_add(result[:], product[:], bias[:, layer : layer + 1])
-            else:
-                nc.scalar.activation(
-                    result[:], product[:], ACT.Identity, bias=bias[:, layer : layer + 1]
+        stores = [(layer, first) for layer in range(LAYERS) for first in range(0, N, 2 * PIECE)]
+        for layer, first in stores:
+            result = staged.tile([P, 2 * PIECE], F32, name="result")
+            for h in range(2):
+                edges = slice(first + h * PIECE, first + (h + 1) * PIECE)
+                half = slice(h * PIECE, (h + 1) * PIECE)
+                picked = window[:].indirect(offsets[:, edges.start // 16 : edges.stop // 16])
+                product = banks.tile([P, PIECE], F32, name="product", tag="bank")
+                nc.tensor.matmul(
+                    product[:], weights[:, layer * P : (layer + 1) * P], picked, start=True, stop=True
                 )
-            nc.sync.dma_start(out[layer * P : (layer + 1) * P, first : first + edges], result[:])
+                if h == 0:
+                    nc.vector.tensor_scalar_add(result[:, half], product[:], bias[:, layer : layer + 1])
+                else:
+                    nc.scalar.activation(
+                        result[:, half], product[:], ACT.Identity, bias=bias[:, layer : layer + 1]
+                    )
+                if (layer, first) in (stores[0], stores[-1]):
+                    nc.sync.dma_start(out[layer * P : (layer + 1) * P, edges], result[:, half])
+            if (layer, first) not in (stores[0], stores[-1]):
+                nc.sync.dma_start(
+                    out[layer * P : (layer + 1) * P, first : first + 2 * PIECE], result[:]
+                )

@@ -55,7 +55,7 @@ def tile_gatv2model_kernel(tc, table, w, b, offs, out):
         def add_up_squares(k):
             sumsq[k] = work.tile([P, CHUNK], F32, name="sumsq")
             for c in range(CHUNK):
-                if (c % 2 == 1) if k in (0, CHUNKS - 1) else (c == CHUNK - 1):
+                if k < CHUNKS - 1 and (c == CHUNK - 1 or (k == 0 and c == 1)):
                     squares_v = work.tile([P, D], F32, name="squares_v")
                     nc.vector.scalar_tensor_tensor(
                         squares_v[:], raw[k][:, c, :], 1.0, raw[k][:, c, :], ALU.mult, ALU.mult,

@@ -8,7 +8,8 @@ ALU = mybir.AluOpType
 P = 128
 S, D, M, N = 4096, 128, 512, 1024
 CHUNK = 4
-CHUNKS = S // (CHUNK * P)
+SIZES = [CHUNK] * (S // (CHUNK * P) - 1) + [CHUNK // 2, CHUNK // 2]
+LAST = len(SIZES) - 1
 PIECE = 256
 LAYERS = M // P
 
@@ -17,20 +18,26 @@ FLOPS = 2 * D * M * N
 
 def tile_gatv2model_kernel(tc, table, w, b, offs, out):
     nc = tc.nc
-    table_chunks = table.rearrange("(k c p) d -> k p c d", c=CHUNK, p=P)
+    table_blocks = table.rearrange("(c p) d -> p c d", p=P)
     b_by_row = b.rearrange("(l p) o -> p (l o)", p=P)
 
     with (
         tc.tile_pool(name="held", bufs=1) as held,
-        tc.tile_pool(name="work", bufs=CHUNKS) as work,
+        tc.tile_pool(name="work", bufs=len(SIZES)) as work,
+        tc.tile_pool(name="scaled", bufs=3) as scaled,
         tc.tile_pool(name="staged", bufs=LAYERS * N // (2 * PIECE)) as staged,
         tc.psum_pool(name="banks", bufs=8) as banks,
     ):
-        raw = [held.tile([P, CHUNK, D], BF16, name=f"raw{k}") for k in range(CHUNKS)]
-        for c in range(CHUNK):
-            nc.sync.dma_start(raw[0][:, c, :], table_chunks[0][:, c, :])
-        for k in range(1, CHUNKS):
-            nc.sync.dma_start(raw[k][:], table_chunks[k])
+        firsts = [sum(SIZES[:k]) for k in range(len(SIZES))]
+        raw = [held.tile([P, n, D], BF16, name=f"raw{k}") for k, n in enumerate(SIZES)]
+        for k, n in enumerate(SIZES):
+            c = 0
+            for blocks in (1, 1, 2) if k == 0 else (n,):
+                nc.sync.dma_start(
+                    raw[k][:, c : c + blocks, :],
+                    table_blocks[:, firsts[k] + c : firsts[k] + c + blocks, :],
+                )
+                c += blocks
         offsets = held.tile([P, N // 16], U16, name="offsets")
         nc.sync.dma_start(offsets[:], offs)
         weights = held.tile([P, M], BF16, name="weights")
@@ -49,13 +56,13 @@ def tile_gatv2model_kernel(tc, table, w, b, offs, out):
         nc.scalar.activation(scratch[:], one[:], ACT.Abs_reciprocal_sqrt)
 
         window = held.tile([P, S], BF16, name="window")
-        sumsq = [None] * CHUNKS
-        turned = [None] * CHUNKS
+        sumsq = [None] * len(SIZES)
+        turned = [None] * len(SIZES)
 
         def add_up_squares(k):
             sumsq[k] = work.tile([P, CHUNK], F32, name="sumsq")
-            for c in range(CHUNK):
-                if k < CHUNKS - 1 and (c == CHUNK - 1 or (k == 0 and c == 1)):
+            for c in range(SIZES[k]):
+                if k < LAST - 1 and (c == CHUNK - 1 or (k == 0 and c == 1)):
                     squares_v = work.tile([P, D], F32, name="squares_v")
                     nc.vector.scalar_tensor_tensor(
                         squares_v[:], raw[k][:, c, :], 1.0, raw[k][:, c, :], ALU.mult, ALU.mult,
@@ -69,15 +76,16 @@ def tile_gatv2model_kernel(tc, table, w, b, offs, out):
                     )
 
         def clip_and_turn(k):
+            n = SIZES[k]
             excess = work.tile([P, CHUNK], F32, name="excess")
-            nc.scalar.activation(excess[:], sumsq[k][:], ACT.Relu, bias=minus_one[:])
+            nc.scalar.activation(excess[:, :n], sumsq[k][:, :n], ACT.Relu, bias=minus_one[:])
             scale = work.tile([P, CHUNK], F32, name="scale")
-            nc.scalar.activation(scale[:], excess[:], ACT.Abs_reciprocal_sqrt, bias=one[:])
-            clipped = work.tile([P, CHUNK, D], BF16, name="clipped")
-            for c in range(CHUNK):
+            nc.scalar.activation(scale[:, :n], excess[:, :n], ACT.Abs_reciprocal_sqrt, bias=one[:])
+            clipped = scaled.tile([P, CHUNK, D], BF16, name="clipped")
+            for c in range(n):
                 nc.vector.tensor_scalar_mul(clipped[:, c, :], raw[k][:, c, :], scale[:, c : c + 1])
-            tiles = 2 if k == CHUNKS - 1 else 1
-            blocks = CHUNK // tiles
+            tiles = 1
+            blocks = n // tiles
             turned[k] = []
             for t in range(tiles):
                 turned_blocks = banks.tile([P, blocks * P], BF16, name="turned_blocks", tag="bank")
@@ -89,15 +97,15 @@ def tile_gatv2model_kernel(tc, table, w, b, offs, out):
                 turned[k].append(turned_blocks)
 
         def fill_window(k):
-            columns = CHUNK * P // len(turned[k])
+            columns = SIZES[k] * P // len(turned[k])
             for t, turned_blocks in enumerate(turned[k]):
-                first = k * CHUNK * P + t * columns
+                first = firsts[k] * P + t * columns
                 nc.vector.tensor_copy(window[:, first : first + columns], turned_blocks[:])
 
-        for i in range(CHUNKS + 2):
-            if i < CHUNKS:
+        for i in range(len(SIZES) + 2):
+            if i < len(SIZES):
                 add_up_squares(i)
-            if 1 <= i <= CHUNKS:
+            if 1 <= i <= len(SIZES):
                 clip_and_turn(i - 1)
             if i >= 2:
                 fill_window(i - 2)

@@ -10,6 +10,7 @@ S, D, M, N = 4096, 128, 512, 1024
 CHUNK = 4
 SIZES = [CHUNK] * (S // (CHUNK * P) - 1) + [CHUNK // 2, CHUNK // 2]
 LAST = len(SIZES) - 1
+WIDE = (LAST - 3, LAST - 2)
 PIECE = 256
 LAYERS = M // P
 
@@ -31,6 +32,10 @@ def tile_gatv2model_kernel(tc, table, w, b, offs, out):
         firsts = [sum(SIZES[:k]) for k in range(len(SIZES))]
         raw = [held.tile([P, n, D], BF16, name=f"raw{k}") for k, n in enumerate(SIZES)]
         for k, n in enumerate(SIZES):
+            if k in WIDE:
+                rows = table[firsts[k] * P : (firsts[k] + n) * P, :]
+                nc.sync.dma_start(raw[k][:], rows.rearrange("(p c) d -> p c d", c=n))
+                continue
             c = 0
             for blocks in (1, 1, 2) if k == 0 else (n,):
                 nc.sync.dma_start(
@@ -100,7 +105,14 @@ def tile_gatv2model_kernel(tc, table, w, b, offs, out):
             columns = SIZES[k] * P // len(turned[k])
             for t, turned_blocks in enumerate(turned[k]):
                 first = firsts[k] * P + t * columns
-                nc.vector.tensor_copy(window[:, first : first + columns], turned_blocks[:])
+                columns_in_order = window[:, first : first + columns]
+                if k in WIDE:
+                    nc.scalar.copy(
+                        columns_in_order.rearrange("d (p c) -> d p c", c=SIZES[k]),
+                        turned_blocks[:].rearrange("d (c p) -> d p c", c=SIZES[k]),
+                    )
+                else:
+                    nc.vector.tensor_copy(columns_in_order, turned_blocks[:])
 
         for i in range(len(SIZES) + 2):
             if i < len(SIZES):

import concourse.masks as masks
import concourse.mybir as mybir

BF16, F32, U16 = mybir.dt.bfloat16, mybir.dt.float32, mybir.dt.uint16
ACT = mybir.ActivationFunctionType
ALU = mybir.AluOpType

P = 128
S, D, M, N = 4096, 128, 512, 1024
CHUNK = 4
SIZES = [CHUNK] * (S // (CHUNK * P) - 1) + [CHUNK // 2, CHUNK // 2]
LAST = len(SIZES) - 1
WIDE = (LAST - 3, LAST - 2)
PIECE = 256
LAYERS = M // P

FLOPS = 2 * D * M * N


def tile_gatv2model_kernel(tc, table, w, b, offs, out):
    nc = tc.nc
    table_blocks = table.rearrange("(c p) d -> p c d", p=P)
    b_by_row = b.rearrange("(l p) o -> p (l o)", p=P)

    with (
        tc.tile_pool(name="held", bufs=1) as held,
        tc.tile_pool(name="work", bufs=len(SIZES)) as work,
        tc.tile_pool(name="scaled", bufs=3) as scaled,
        tc.tile_pool(name="staged", bufs=LAYERS * N // (2 * PIECE)) as staged,
        tc.psum_pool(name="banks", bufs=8) as banks,
    ):
        firsts = [sum(SIZES[:k]) for k in range(len(SIZES))]
        raw = [held.tile([P, n, D], BF16, name=f"raw{k}") for k, n in enumerate(SIZES)]
        for k, n in enumerate(SIZES):
            if k in WIDE:
                rows = table[firsts[k] * P : (firsts[k] + n) * P, :]
                nc.sync.dma_start(raw[k][:], rows.rearrange("(p c) d -> p c d", c=n))
                continue
            c = 0
            for blocks in (1, 1, 2) if k == 0 else (n,):
                nc.sync.dma_start(
                    raw[k][:, c : c + blocks, :],
                    table_blocks[:, firsts[k] + c : firsts[k] + c + blocks, :],
                )
                c += blocks
        offsets = held.tile([P, N // 16], U16, name="offsets")
        nc.sync.dma_start(offsets[:], offs)
        weights = held.tile([P, M], BF16, name="weights")
        nc.sync.dma_start(weights[:], w)
        bias = held.tile([P, LAYERS], F32, name="bias")
        nc.sync.dma_start(bias[:], b_by_row)

        identity = held.tile([P, P], BF16, name="identity")
        masks.make_identity(nc, identity[:])

        one = held.tile([P, 1], F32, name="one")
        nc.vector.memset(one[:], 1.0)
        minus_one = held.tile([P, 1], F32, name="minus_one")
        nc.vector.memset(minus_one[:], -1.0)
        scratch = held.tile([P, 1], F32, name="scratch")
        nc.scalar.activation(scratch[:], one[:], ACT.Abs_reciprocal_sqrt)

        window = held.tile([P, S], BF16, name="window")
        sumsq = [None] * len(SIZES)
        turned = [None] * len(SIZES)

        def add_up_squares(k):
            sumsq[k] = work.tile([P, CHUNK], F32, name="sumsq")
            for c in range(SIZES[k]):
                if k < LAST - 1 and (c == CHUNK - 1 or (k == 0 and c == 1)):
                    squares_v = work.tile([P, D], F32, name="squares_v")
                    nc.vector.scalar_tensor_tensor(
                        squares_v[:], raw[k][:, c, :], 1.0, raw[k][:, c, :], ALU.mult, ALU.mult,
                        accum_out=sumsq[k][:, c : c + 1],
                    )
                else:
                    squares_s = work.tile([P, D], BF16, name="squares_s")
                    nc.scalar.activation(
                        squares_s[:], raw[k][:, c, :], ACT.Square,
                        accum_out=sumsq[k][:, c : c + 1],
                    )

        def clip_and_turn(k):
            n = SIZES[k]
            excess = work.tile([P, CHUNK], F32, name="excess")
            nc.scalar.activation(excess[:, :n], sumsq[k][:, :n], ACT.Relu, bias=minus_one[:])
            scale = work.tile([P, CHUNK], F32, name="scale")
            nc.scalar.activation(scale[:, :n], excess[:, :n], ACT.Abs_reciprocal_sqrt, bias=one[:])
            clipped = scaled.tile([P, CHUNK, D], BF16, name="clipped")
            for c in range(n):
                nc.vector.tensor_scalar_mul(clipped[:, c, :], raw[k][:, c, :], scale[:, c : c + 1])
            tiles = 1
            blocks = n // tiles
            turned[k] = []
            for t in range(tiles):
                turned_blocks = banks.tile([P, blocks * P], BF16, name="turned_blocks", tag="bank")
                for c in range(blocks):
                    nc.tensor.matmul(
                        turned_blocks[:, c * P : (c + 1) * P], clipped[:, t * blocks + c, :],
                        identity[:], start=True, stop=True,
                    )
                turned[k].append(turned_blocks)

        def fill_window(k):
            columns = SIZES[k] * P // len(turned[k])
            for t, turned_blocks in enumerate(turned[k]):
                first = firsts[k] * P + t * columns
                columns_in_order = window[:, first : first + columns]
                if k in WIDE:
                    nc.scalar.copy(
                        columns_in_order.rearrange("d (p c) -> d p c", c=SIZES[k]),
                        turned_blocks[:].rearrange("d (c p) -> d p c", c=SIZES[k]),
                    )
                else:
                    nc.vector.tensor_copy(columns_in_order, turned_blocks[:])

        for i in range(len(SIZES) + 2):
            if i < len(SIZES):
                add_up_squares(i)
            if 1 <= i <= len(SIZES):
                clip_and_turn(i - 1)
            if i >= 2:
                fill_window(i - 2)

        stores = [(layer, first) for layer in range(LAYERS) for first in range(0, N, 2 * PIECE)]
        for layer, first in stores:
            result = staged.tile([P, 2 * PIECE], F32, name="result")
            for h in range(2):
                edges = slice(first + h * PIECE, first + (h + 1) * PIECE)
                half = slice(h * PIECE, (h + 1) * PIECE)
                picked = window[:].indirect(offsets[:, edges.start // 16 : edges.stop // 16])
                product = banks.tile([P, PIECE], F32, name="product", tag="bank")
                nc.tensor.matmul(
                    product[:], weights[:, layer * P : (layer + 1) * P], picked, start=True, stop=True
                )
                if h == 0:
                    nc.vector.tensor_scalar_add(result[:, half], product[:], bias[:, layer : layer + 1])
                else:
                    nc.scalar.activation(
                        result[:, half], product[:], ACT.Identity, bias=bias[:, layer : layer + 1]
                    )
                if (layer, first) in (stores[0], stores[-1]):
                    nc.sync.dma_start(out[layer * P : (layer + 1) * P, edges], result[:, half])
            if (layer, first) not in (stores[0], stores[-1]):
                nc.sync.dma_start(
                    out[layer * P : (layer + 1) * P, first : first + 2 * PIECE], result[:]
                )
